import numpy as np
import ml_dtypes


def mxq(x, axis, fmt="e4m3"):
    dtype, down = {"e4m3": (ml_dtypes.float8_e4m3fn, 7), "e5m2": (ml_dtypes.float8_e5m2, 14)}[fmt]
    v = np.moveaxis(np.asarray(x, np.float32).astype(ml_dtypes.bfloat16).astype(np.float64), axis, -1)
    blocks = v.reshape(v.shape[:-1] + (-1, 32))
    amax = np.abs(blocks).max(-1, keepdims=True)
    byte = np.maximum(np.where(amax > 0, np.frexp(amax)[1] - 1 + 127, 0) - down, 1)
    scale = np.exp2(byte - 127.0)
    codes = (blocks / scale).astype(np.float32).astype(dtype).astype(np.float64)
    return np.moveaxis((codes * scale).reshape(v.shape), -1, axis)


WIDE = False


def mx_kscale(k):
    if not WIDE:
        return np.ones(k)
    levels = np.array([20, -20, 10, -10, 0])
    a = np.random.permutation(np.resize(levels, k // 512 * 4)).reshape(k // 512, 4)
    idx = np.arange(k)
    return np.exp2(a[idx // 512, idx % 128 // 32])


BF16 = ml_dtypes.bfloat16


def bf(x):
    return np.asarray(x, np.float32).astype(BF16)


def f64(x):
    return np.asarray(x).astype(np.float64)


N1, N2, N3, R1, R = 32, 32, 512, 512, 512


def setup_inputs():
    s = mx_kscale(N1 * N2)[::N2]
    g = R ** (-1.0 / 6.0)
    X = np.random.standard_normal((N1, N2, N3))
    A = np.random.standard_normal((N1, R)) * g * s[:, None]
    B = np.random.standard_normal((N2, R)) * g
    C = np.random.standard_normal((N3, R)) * g
    go = np.random.standard_normal((N1, N2, N3)) * np.exp2(np.random.randint(-12, 1, (N1, N2, 1))) * 4.0 / s[:, None, None]
    return {"X": bf(X), "A": bf(A), "B": bf(B), "C": bf(C), "grad_out": bf(go)}


def reference(X, A, B, C, grad_out):
    p = (f64(A)[:, None, :] * f64(B)[None, :, :]).reshape(N1 * N2, R)
    g = f64(grad_out).reshape(N1 * N2, N3)
    return mxq(g, 0, "e5m2").T @ mxq(p, 0, "e4m3")

@@ -1,0 +1,106 @@
+from contextlib import ExitStack
+
+import concourse.mybir as mybir
+
+BF16 = mybir.dt.bfloat16
+F32 = mybir.dt.float32
+U32 = mybir.dt.uint32
+U8 = mybir.dt.uint8
+E4M3_X4 = mybir.dt.float8_e4m3fn_x4
+E5M2_X4 = mybir.dt.float8_e5m2_x4
+
+N1, N2, N3, R = 32, 32, 512, 512
+P = 128
+PACK = 4
+K_PASS = P * PACK
+PASSES = N1 * N2 // K_PASS
+BLOCK_PARTITIONS = 8
+I_PER_PASS = P // BLOCK_PARTITIONS
+M_TILE = 128
+M_TILES = N3 // M_TILE
+
+FLOPS = 2 * N1 * N2 * N3 * R
+BYTES = 2 * (N1 * R + N2 * R + N1 * N2 * N3) + 4 * N3 * R
+
+
+def tile_recon_loss_pa_s_kernel(tc, X, A, B, C, grad_out, out):
+    nc = tc.nc
+    g_rows = grad_out.rearrange("i j k -> (i j) k")
+
+    with ExitStack() as ctx:
+        keep = ctx.enter_context(tc.tile_pool(name="keep", bufs=1))
+        psum = ctx.enter_context(tc.psum_pool(name="psum", bufs=1))
+
+        b_rep = keep.tile([P, PACK, R], BF16)
+        nc.sync.dma_start(
+            out=b_rep[:].rearrange("p t r -> p (t r)"),
+            in_=B.rearrange("(s t) r -> s (t r)", t=PACK)
+            .unsqueeze(0)
+            .to_broadcast([I_PER_PASS, BLOCK_PARTITIONS, PACK * R]),
+        )
+        a_rep = []
+        g_raw = []
+        for c in range(PASSES):
+            a_rep.append(keep.tile([P, R], BF16, name="a_rep%d" % c))
+            nc.sync.dma_start(
+                out=a_rep[c][:],
+                in_=A[c * I_PER_PASS : (c + 1) * I_PER_PASS, :]
+                .unsqueeze(1)
+                .to_broadcast([I_PER_PASS, BLOCK_PARTITIONS, R]),
+            )
+            g_raw.append(keep.tile([P, PACK, N3], BF16, name="g_raw%d" % c))
+            nc.sync.dma_start(
+                out=g_raw[c][:],
+                in_=g_rows[c * K_PASS : (c + 1) * K_PASS, :].rearrange("(p t) k -> p t k", t=PACK),
+            )
+
+        acc = [psum.tile([M_TILE, R], F32, name="acc%d" % m) for m in range(M_TILES)]
+
+        for c in range(PASSES):
+            p_grouped = keep.tile([P, R, PACK], BF16, name="p_grouped%d" % c, align_bytes=64)
+            nc.vector.tensor_tensor(
+                out=p_grouped[:],
+                in0=a_rep[c][:].unsqueeze(2).to_broadcast([P, R, PACK]),
+                in1=b_rep[:].rearrange("p t r -> p r t"),
+                op=mybir.AluOpType.mult,
+            )
+            g_grouped = keep.tile([P, N3, PACK], BF16, name="g_grouped%d" % c, align_bytes=64)
+            nc.scalar.copy(
+                out=g_grouped[:].rearrange("p (n i) t -> p n t i", i=4),
+                in_=g_raw[c][:].rearrange("p t (n i) -> p n t i", i=4),
+            )
+
+            p_codes = keep.tile([P, R], U32, name="p_codes%d" % c, align_bytes=64)
+            p_scales = keep.tile([P, R], U8, name="p_scales%d" % c, align_bytes=64)
+            nc.vector.quantize_mx(
+                out=p_codes[:].bitcast(E4M3_X4),
+                scales=p_scales[:],
+                in_=p_grouped[:].rearrange("p r t -> p (r t)"),
+            )
+            g_codes = keep.tile([P, N3], U32, name="g_codes%d" % c, align_bytes=64)
+            g_scales = keep.tile([P, N3], U8, name="g_scales%d" % c, align_bytes=64)
+            nc.vector.quantize_mx(
+                out=g_codes[:].bitcast(E5M2_X4),
+                scales=g_scales[:],
+                in_=g_grouped[:].rearrange("p k t -> p (k t)"),
+            )
+
+            for m in range(M_TILES):
+                m_cols = slice(m * M_TILE, (m + 1) * M_TILE)
+                nc.tensor.matmul_mx(
+                    out=acc[m][:],
+                    lhsT=g_codes[:, m_cols].bitcast(E5M2_X4),
+                    lhsT_scale=g_scales[:, m_cols],
+                    rhs=p_codes[:].bitcast(E4M3_X4),
+                    rhs_scale=p_scales[:],
+                    start=(c == 0),
+                    stop=(c == PASSES - 1),
+                )
+
+        for m in range(M_TILES):
+            result = keep.tile([M_TILE, R], F32, name="result%d" % m)
+            if m % 2 == 0:
+                nc.scalar.copy(out=result[:], in_=acc[m][:])
+            else:
+                nc.vector.tensor_copy(out=result[:], in_=acc[m][:])
+            nc.sync.dma_start(out=out[m * M_TILE : (m + 1) * M_TILE, :], in_=result[:])

@@ -18,6 +18,8 @@ BLOCK_PARTITIONS = 8
 I_PER_PASS = P // BLOCK_PARTITIONS
 M_TILE = 128
 M_TILES = N3 // M_TILE
+HALVES = 2
+R_HALF = R // HALVES
 
 FLOPS = 2 * N1 * N2 * N3 * R
 BYTES = 2 * (N1 * R + N2 * R + N1 * N2 * N3) + 4 * N3 * R
@@ -30,77 +32,117 @@ def tile_recon_loss_pa_s_kernel(tc, X, A, B, C, grad_out, out):
     with ExitStack() as ctx:
         keep = ctx.enter_context(tc.tile_pool(name="keep", bufs=1))
         psum = ctx.enter_context(tc.psum_pool(name="psum", bufs=1))
+        ctx.enter_context(tc.manual_schedule())
 
-        b_rep = keep.tile([P, PACK, R], BF16)
-        nc.sync.dma_start(
-            out=b_rep[:].rearrange("p t r -> p (t r)"),
-            in_=B.rearrange("(s t) r -> s (t r)", t=PACK)
-            .unsqueeze(0)
-            .to_broadcast([I_PER_PASS, BLOCK_PARTITIONS, PACK * R]),
-        )
-        a_rep = []
-        g_raw = []
-        for c in range(PASSES):
-            a_rep.append(keep.tile([P, R], BF16, name="a_rep%d" % c))
+        b_rep = [keep.tile([P, PACK, R_HALF], BF16, name="b_rep%d" % h) for h in range(HALVES)]
+        a_rep = [keep.tile([P, R], BF16, name="a_rep%d" % c) for c in range(PASSES)]
+        g_raw = [keep.tile([P, PACK, N3], BF16, name="g_raw%d" % c) for c in range(PASSES)]
+        p_grouped = [
+            keep.tile([P, R, PACK], BF16, name="p_grouped%d" % c, align_bytes=64) for c in range(PASSES)
+        ]
+        g_grouped = [
+            keep.tile([P, N3, PACK], BF16, name="g_grouped%d" % c, align_bytes=64) for c in range(PASSES)
+        ]
+        p_codes = [keep.tile([P, R], U32, name="p_codes%d" % c, align_bytes=64) for c in range(PASSES)]
+        p_scales = [keep.tile([P, R], U8, name="p_scales%d" % c, align_bytes=64) for c in range(PASSES)]
+        g_codes = [keep.tile([P, N3], U32, name="g_codes%d" % c, align_bytes=64) for c in range(PASSES)]
+        g_scales = [keep.tile([P, N3], U8, name="g_scales%d" % c, align_bytes=64) for c in range(PASSES)]
+        acc = [psum.tile([M_TILE, R], F32, name="acc%d" % m) for m in range(M_TILES)]
+        result = [keep.tile([M_TILE, R], F32, name="result%d" % m) for m in range(M_TILES)]
+
+        def load_b(h):
+            nc.sync.dma_start(
+                out=b_rep[h][:],
+                in_=B[:, h * R_HALF : (h + 1) * R_HALF]
+                .rearrange("(s t) r -> s t r", t=PACK)
+                .unsqueeze(0)
+                .to_broadcast([I_PER_PASS, BLOCK_PARTITIONS, PACK, R_HALF]),
+            )
+
+        def load_a(c):
             nc.sync.dma_start(
                 out=a_rep[c][:],
                 in_=A[c * I_PER_PASS : (c + 1) * I_PER_PASS, :]
                 .unsqueeze(1)
                 .to_broadcast([I_PER_PASS, BLOCK_PARTITIONS, R]),
             )
-            g_raw.append(keep.tile([P, PACK, N3], BF16, name="g_raw%d" % c))
+
+        def load_g(c):
             nc.sync.dma_start(
                 out=g_raw[c][:],
                 in_=g_rows[c * K_PASS : (c + 1) * K_PASS, :].rearrange("(p t) k -> p t k", t=PACK),
             )
 
-        acc = [psum.tile([M_TILE, R], F32, name="acc%d" % m) for m in range(M_TILES)]
-
-        for c in range(PASSES):
-            p_grouped = keep.tile([P, R, PACK], BF16, name="p_grouped%d" % c, align_bytes=64)
+        def make_p(c, h):
+            r_cols = slice(h * R_HALF, (h + 1) * R_HALF)
             nc.vector.tensor_tensor(
-                out=p_grouped[:],
-                in0=a_rep[c][:].unsqueeze(2).to_broadcast([P, R, PACK]),
-                in1=b_rep[:].rearrange("p t r -> p r t"),
+                out=p_grouped[c][:, r_cols, :],
+                in0=a_rep[c][:, r_cols].unsqueeze(2).to_broadcast([P, R_HALF, PACK]),
+                in1=b_rep[h][:].rearrange("p t r -> p r t"),
                 op=mybir.AluOpType.mult,
             )
-            g_grouped = keep.tile([P, N3, PACK], BF16, name="g_grouped%d" % c, align_bytes=64)
+
+        def quantise_p(c):
+            nc.vector.quantize_mx(
+                out=p_codes[c][:].bitcast(E4M3_X4),
+                scales=p_scales[c][:],
+                in_=p_grouped[c][:].rearrange("p r t -> p (r t)"),
+            )
+
+        def regroup_g(c, m):
+            m_cols = slice(m * M_TILE, (m + 1) * M_TILE)
             nc.scalar.copy(
-                out=g_grouped[:].rearrange("p (n i) t -> p n t i", i=4),
-                in_=g_raw[c][:].rearrange("p t (n i) -> p n t i", i=4),
+                out=g_grouped[c][:, m_cols, :].rearrange("p (n i) t -> p n t i", i=4),
+                in_=g_raw[c][:, :, m_cols].rearrange("p t (n i) -> p n t i", i=4),
             )
 
-            p_codes = keep.tile([P, R], U32, name="p_codes%d" % c, align_bytes=64)
-            p_scales = keep.tile([P, R], U8, name="p_scales%d" % c, align_bytes=64)
+        def quantise_g(c, m):
+            m_cols = slice(m * M_TILE, (m + 1) * M_TILE)
             nc.vector.quantize_mx(
-                out=p_codes[:].bitcast(E4M3_X4),
-                scales=p_scales[:],
-                in_=p_grouped[:].rearrange("p r t -> p (r t)"),
-            )
-            g_codes = keep.tile([P, N3], U32, name="g_codes%d" % c, align_bytes=64)
-            g_scales = keep.tile([P, N3], U8, name="g_scales%d" % c, align_bytes=64)
-            nc.vector.quantize_mx(
-                out=g_codes[:].bitcast(E5M2_X4),
-                scales=g_scales[:],
-                in_=g_grouped[:].rearrange("p k t -> p (k t)"),
+                out=g_codes[c][:, m_cols].bitcast(E5M2_X4),
+                scales=g_scales[c][:, m_cols],
+                in_=g_grouped[c][:, m_cols, :].rearrange("p k t -> p (k t)"),
             )
 
+        def multiply(c, m):
+            m_cols = slice(m * M_TILE, (m + 1) * M_TILE)
+            nc.tensor.matmul_mx(
+                out=acc[m][:],
+                lhsT=g_codes[c][:, m_cols].bitcast(E5M2_X4),
+                lhsT_scale=g_scales[c][:, m_cols],
+                rhs=p_codes[c][:].bitcast(E4M3_X4),
+                rhs_scale=p_scales[c][:],
+                start=(c == 0),
+                stop=(c == PASSES - 1),
+            )
+
+        load_b(0)
+        load_a(0)
+        load_b(1)
+        load_a(1)
+        load_g(0)
+        load_g(1)
+
+        for c in range(PASSES):
             for m in range(M_TILES):
-                m_cols = slice(m * M_TILE, (m + 1) * M_TILE)
-                nc.tensor.matmul_mx(
-                    out=acc[m][:],
-                    lhsT=g_codes[:, m_cols].bitcast(E5M2_X4),
-                    lhsT_scale=g_scales[:, m_cols],
-                    rhs=p_codes[:].bitcast(E4M3_X4),
-                    rhs_scale=p_scales[:],
-                    start=(c == 0),
-                    stop=(c == PASSES - 1),
-                )
+                regroup_g(c, m)
+
+        make_p(0, 0)
+        make_p(0, 1)
+        make_p(1, 0)
+        quantise_p(0)
+        for m in range(M_TILES):
+            quantise_g(0, m)
+            multiply(0, m)
+        make_p(1, 1)
+        quantise_p(1)
+        for m in range(M_TILES):
+            quantise_g(1, m)
+            multiply(1, m)
 
         for m in range(M_TILES):
-            result = keep.tile([M_TILE, R], F32, name="result%d" % m)
             if m % 2 == 0:
-                nc.scalar.copy(out=result[:], in_=acc[m][:])
+                nc.scalar.copy(out=result[m][:], in_=acc[m][:])
             else:
-                nc.vector.tensor_copy(out=result[:], in_=acc[m][:])
-            nc.sync.dma_start(out=out[m * M_TILE : (m + 1) * M_TILE, :], in_=result[:])
+                nc.vector.tensor_copy(out=result[m][:], in_=acc[m][:])
+            nc.sync.dma_start(out=out[m * M_TILE : (m + 1) * M_TILE, :], in_=result[m][:])

@@ -34,14 +34,16 @@ def tile_recon_loss_pa_s_kernel(tc, X, A, B, C, grad_out, out):
         psum = ctx.enter_context(tc.psum_pool(name="psum", bufs=1))
         ctx.enter_context(tc.manual_schedule())
 
-        b_rep = [keep.tile([P, PACK, R_HALF], BF16, name="b_rep%d" % h) for h in range(HALVES)]
         a_rep = [keep.tile([P, R], BF16, name="a_rep%d" % c) for c in range(PASSES)]
+        a_pairs = [keep.tile([P, R, 2], BF16, name="a_pairs%d" % c) for c in range(PASSES)]
+        b_rep = [keep.tile([P, PACK, R_HALF], BF16, name="b_rep%d" % h) for h in range(HALVES)]
+        b_grouped = [keep.tile([P, R_HALF, PACK], BF16, name="b_grouped%d" % h) for h in range(HALVES)]
         g_raw = [keep.tile([P, PACK, N3], BF16, name="g_raw%d" % c) for c in range(PASSES)]
-        p_grouped = [
-            keep.tile([P, R, PACK], BF16, name="p_grouped%d" % c, align_bytes=64) for c in range(PASSES)
-        ]
         g_grouped = [
             keep.tile([P, N3, PACK], BF16, name="g_grouped%d" % c, align_bytes=64) for c in range(PASSES)
+        ]
+        p_grouped = [
+            keep.tile([P, R, PACK], BF16, name="p_grouped%d" % c, align_bytes=64) for c in range(PASSES)
         ]
         p_codes = [keep.tile([P, R], U32, name="p_codes%d" % c, align_bytes=64) for c in range(PASSES)]
         p_scales = [keep.tile([P, R], U8, name="p_scales%d" % c, align_bytes=64) for c in range(PASSES)]
@@ -49,6 +51,14 @@ def tile_recon_loss_pa_s_kernel(tc, X, A, B, C, grad_out, out):
         g_scales = [keep.tile([P, N3], U8, name="g_scales%d" % c, align_bytes=64) for c in range(PASSES)]
         acc = [psum.tile([M_TILE, R], F32, name="acc%d" % m) for m in range(M_TILES)]
         result = [keep.tile([M_TILE, R], F32, name="result%d" % m) for m in range(M_TILES)]
+
+        def load_a(c):
+            nc.sync.dma_start(
+                out=a_rep[c][:],
+                in_=A[c * I_PER_PASS : (c + 1) * I_PER_PASS, :]
+                .unsqueeze(1)
+                .to_broadcast([I_PER_PASS, BLOCK_PARTITIONS, R]),
+            )
 
         def load_b(h):
             nc.sync.dma_start(
@@ -59,26 +69,29 @@ def tile_recon_loss_pa_s_kernel(tc, X, A, B, C, grad_out, out):
                 .to_broadcast([I_PER_PASS, BLOCK_PARTITIONS, PACK, R_HALF]),
             )
 
-        def load_a(c):
-            nc.sync.dma_start(
-                out=a_rep[c][:],
-                in_=A[c * I_PER_PASS : (c + 1) * I_PER_PASS, :]
-                .unsqueeze(1)
-                .to_broadcast([I_PER_PASS, BLOCK_PARTITIONS, R]),
-            )
-
         def load_g(c):
             nc.sync.dma_start(
                 out=g_raw[c][:],
                 in_=g_rows[c * K_PASS : (c + 1) * K_PASS, :].rearrange("(p t) k -> p t k", t=PACK),
             )
 
+        def regroup(copy, grouped, raw):
+            copy(
+                out=grouped.rearrange("p (n i) t -> p n t i", i=4),
+                in_=raw.rearrange("p t (n i) -> p n t i", i=4),
+            )
+
+        def regroup_g(c, m):
+            m_cols = slice(m * M_TILE, (m + 1) * M_TILE)
+            copy = nc.scalar.copy if m < M_TILES - 1 else nc.vector.tensor_copy
+            regroup(copy, g_grouped[c][:, m_cols, :], g_raw[c][:, :, m_cols])
+
         def make_p(c, h):
             r_cols = slice(h * R_HALF, (h + 1) * R_HALF)
             nc.vector.tensor_tensor(
-                out=p_grouped[c][:, r_cols, :],
-                in0=a_rep[c][:, r_cols].unsqueeze(2).to_broadcast([P, R_HALF, PACK]),
-                in1=b_rep[h][:].rearrange("p t r -> p r t"),
+                out=p_grouped[c][:, r_cols, :].rearrange("p r (u e) -> p r u e", e=2),
+                in0=a_pairs[c][:, r_cols, :].unsqueeze(2).to_broadcast([P, R_HALF, PACK // 2, 2]),
+                in1=b_grouped[h][:].rearrange("p r (u e) -> p r u e", e=2),
                 op=mybir.AluOpType.mult,
             )
 
@@ -87,13 +100,6 @@ def tile_recon_loss_pa_s_kernel(tc, X, A, B, C, grad_out, out):
                 out=p_codes[c][:].bitcast(E4M3_X4),
                 scales=p_scales[c][:],
                 in_=p_grouped[c][:].rearrange("p r t -> p (r t)"),
-            )
-
-        def regroup_g(c, m):
-            m_cols = slice(m * M_TILE, (m + 1) * M_TILE)
-            nc.scalar.copy(
-                out=g_grouped[c][:, m_cols, :].rearrange("p (n i) t -> p n t i", i=4),
-                in_=g_raw[c][:, :, m_cols].rearrange("p t (n i) -> p n t i", i=4),
             )
 
         def quantise_g(c, m):
@@ -116,29 +122,27 @@ def tile_recon_loss_pa_s_kernel(tc, X, A, B, C, grad_out, out):
                 stop=(c == PASSES - 1),
             )
 
-        load_b(0)
         load_a(0)
+        load_b(0)
         load_b(1)
         load_a(1)
         load_g(0)
         load_g(1)
 
         for c in range(PASSES):
+            nc.scalar.copy(out=a_pairs[c][:], in_=a_rep[c][:].unsqueeze(2).to_broadcast([P, R, 2]))
+        for h in range(HALVES):
+            regroup(nc.vector.tensor_copy, b_grouped[h][:], b_rep[h][:])
+
+        for c in range(PASSES):
+            for h in range(HALVES):
+                make_p(c, h)
             for m in range(M_TILES):
                 regroup_g(c, m)
-
-        make_p(0, 0)
-        make_p(0, 1)
-        make_p(1, 0)
-        quantise_p(0)
-        for m in range(M_TILES):
-            quantise_g(0, m)
-            multiply(0, m)
-        make_p(1, 1)
-        quantise_p(1)
-        for m in range(M_TILES):
-            quantise_g(1, m)
-            multiply(1, m)
+            quantise_p(c)
+            for m in range(M_TILES):
+                quantise_g(c, m)
+                multiply(c, m)
 
         for m in range(M_TILES):
             if m % 2 == 0:

@@ -83,7 +83,7 @@ def tile_recon_loss_pa_s_kernel(tc, X, A, B, C, grad_out, out):
 
         def regroup_g(c, m):
             m_cols = slice(m * M_TILE, (m + 1) * M_TILE)
-            copy = nc.scalar.copy if m < M_TILES - 1 else nc.vector.tensor_copy
+            copy = nc.vector.tensor_copy if c == 0 and m == M_TILES - 1 else nc.scalar.copy
             regroup(copy, g_grouped[c][:, m_cols, :], g_raw[c][:, :, m_cols])
 
         def make_p(c, h):
@@ -95,11 +95,12 @@ def tile_recon_loss_pa_s_kernel(tc, X, A, B, C, grad_out, out):
                 op=mybir.AluOpType.mult,
             )
 
-        def quantise_p(c):
+        def quantise_p(c, h):
+            r_cols = slice(h * R_HALF, (h + 1) * R_HALF)
             nc.vector.quantize_mx(
-                out=p_codes[c][:].bitcast(E4M3_X4),
-                scales=p_scales[c][:],
-                in_=p_grouped[c][:].rearrange("p r t -> p (r t)"),
+                out=p_codes[c][:, r_cols].bitcast(E4M3_X4),
+                scales=p_scales[c][:, r_cols],
+                in_=p_grouped[c][:, r_cols, :].rearrange("p r t -> p (r t)"),
             )
 
         def quantise_g(c, m):
@@ -139,14 +140,15 @@ def tile_recon_loss_pa_s_kernel(tc, X, A, B, C, grad_out, out):
                 make_p(c, h)
             for m in range(M_TILES):
                 regroup_g(c, m)
-            quantise_p(c)
+            for h in range(HALVES):
+                quantise_p(c, h)
             for m in range(M_TILES):
                 quantise_g(c, m)
                 multiply(c, m)
 
         for m in range(M_TILES):
-            if m % 2 == 0:
-                nc.scalar.copy(out=result[m][:], in_=acc[m][:])
-            else:
-                nc.vector.tensor_copy(out=result[m][:], in_=acc[m][:])
-            nc.sync.dma_start(out=out[m * M_TILE : (m + 1) * M_TILE, :], in_=result[m][:])
+            copy = nc.scalar.copy if m % 2 == 0 else nc.vector.tensor_copy
+            for h in range(HALVES):
+                r_cols = slice(h * R_HALF, (h + 1) * R_HALF)
+                copy(out=result[m][:, r_cols], in_=acc[m][:, r_cols])
+                nc.sync.dma_start(out=out[m * M_TILE : (m + 1) * M_TILE, r_cols], in_=result[m][:, r_cols])

@@ -20,6 +20,7 @@ M_TILE = 128
 M_TILES = N3 // M_TILE
 HALVES = 2
 R_HALF = R // HALVES
+R_QUARTER = R // 4
 
 FLOPS = 2 * N1 * N2 * N3 * R
 BYTES = 2 * (N1 * R + N2 * R + N1 * N2 * N3) + 4 * N3 * R
@@ -36,8 +37,11 @@ def tile_recon_loss_pa_s_kernel(tc, X, A, B, C, grad_out, out):
 
         a_rep = [keep.tile([P, R], BF16, name="a_rep%d" % c) for c in range(PASSES)]
         a_pairs = [keep.tile([P, R, 2], BF16, name="a_pairs%d" % c) for c in range(PASSES)]
-        b_rep = [keep.tile([P, PACK, R_HALF], BF16, name="b_rep%d" % h) for h in range(HALVES)]
-        b_grouped = [keep.tile([P, R_HALF, PACK], BF16, name="b_grouped%d" % h) for h in range(HALVES)]
+        b_rep = keep.tile([P, PACK, R_QUARTER], BF16, name="b_rep")
+        b_rows = keep.tile([P, PACK, R_QUARTER], BF16, name="b_rows")
+        sel = keep.tile([P, 3 * P], BF16, name="sel")
+        b_first = keep.tile([P, R_QUARTER, PACK], BF16, name="b_first")
+        b_psum = [psum.tile([P, R_HALF, PACK], BF16, name="b_psum%d" % w) for w in range(1, 4)]
         g_raw = [keep.tile([P, PACK, N3], BF16, name="g_raw%d" % c) for c in range(PASSES)]
         g_grouped = [
             keep.tile([P, N3, PACK], BF16, name="g_grouped%d" % c, align_bytes=64) for c in range(PASSES)
@@ -60,14 +64,17 @@ def tile_recon_loss_pa_s_kernel(tc, X, A, B, C, grad_out, out):
                 .to_broadcast([I_PER_PASS, BLOCK_PARTITIONS, R]),
             )
 
-        def load_b(h):
+        def load_b_first_quarter():
             nc.sync.dma_start(
-                out=b_rep[h][:],
-                in_=B[:, h * R_HALF : (h + 1) * R_HALF]
+                out=b_rep[:],
+                in_=B[:, 0:R_QUARTER]
                 .rearrange("(s t) r -> s t r", t=PACK)
                 .unsqueeze(0)
-                .to_broadcast([I_PER_PASS, BLOCK_PARTITIONS, PACK, R_HALF]),
+                .to_broadcast([I_PER_PASS, BLOCK_PARTITIONS, PACK, R_QUARTER]),
             )
+
+        def load_b_rows():
+            nc.sync.dma_start(out=b_rows[0:32], in_=B.rearrange("(s t) (w r) -> w s t r", t=PACK, w=4))
 
         def load_g(c):
             nc.sync.dma_start(
@@ -81,18 +88,33 @@ def tile_recon_loss_pa_s_kernel(tc, X, A, B, C, grad_out, out):
                 in_=raw.rearrange("p t (n i) -> p n t i", i=4),
             )
 
-        def regroup_g(c, m):
+        def regroup_g(copy, c, m):
             m_cols = slice(m * M_TILE, (m + 1) * M_TILE)
-            copy = nc.vector.tensor_copy if c == 0 and m == M_TILES - 1 else nc.scalar.copy
             regroup(copy, g_grouped[c][:, m_cols, :], g_raw[c][:, :, m_cols])
 
-        def make_p(c, h):
-            r_cols = slice(h * R_HALF, (h + 1) * R_HALF)
+        def regroup_b_on_tensor(w):
+            nc.tensor.matmul(
+                out=b_psum[w - 1][:, 0:R_QUARTER, :],
+                lhsT=sel[:, (w - 1) * P : w * P],
+                rhs=b_rows[:].rearrange("p t r -> p r t"),
+                start=True,
+                stop=True,
+            )
+
+        def make_p(c, w):
+            r_cols = slice(w * R_QUARTER, (w + 1) * R_QUARTER)
+            b_grouped = b_first[:] if w == 0 else b_psum[w - 1][:, 0:R_QUARTER, :]
             nc.vector.tensor_tensor(
                 out=p_grouped[c][:, r_cols, :].rearrange("p r (u e) -> p r u e", e=2),
-                in0=a_pairs[c][:, r_cols, :].unsqueeze(2).to_broadcast([P, R_HALF, PACK // 2, 2]),
-                in1=b_grouped[h][:].rearrange("p r (u e) -> p r u e", e=2),
+                in0=a_pairs[c][:, r_cols, :].unsqueeze(2).to_broadcast([P, R_QUARTER, PACK // 2, 2]),
+                in1=b_grouped.rearrange("p r (u e) -> p r u e", e=2),
                 op=mybir.AluOpType.mult,
+            )
+
+        def double_a(copy, c, h):
+            r_cols = slice(h * R_HALF, (h + 1) * R_HALF)
+            copy(
+                out=a_pairs[c][:, r_cols, :], in_=a_rep[c][:, r_cols].unsqueeze(2).to_broadcast([P, R_HALF, 2])
             )
 
         def quantise_p(c, h):
@@ -124,31 +146,70 @@ def tile_recon_loss_pa_s_kernel(tc, X, A, B, C, grad_out, out):
             )
 
         load_a(0)
-        load_b(0)
-        load_b(1)
+        load_b_rows()
+        load_b_first_quarter()
         load_a(1)
         load_g(0)
         load_g(1)
 
-        for c in range(PASSES):
-            nc.scalar.copy(out=a_pairs[c][:], in_=a_rep[c][:].unsqueeze(2).to_broadcast([P, R, 2]))
-        for h in range(HALVES):
-            regroup(nc.vector.tensor_copy, b_grouped[h][:], b_rep[h][:])
+        on_scalar, on_vector = nc.scalar.copy, nc.vector.tensor_copy
+
+        nc.vector.memset(b_rows[32:64], 0.0)
+        nc.vector.memset(b_rows[64:128], 0.0)
+        nc.gpsimd.memset(sel[:], 1.0)
+        nc.gpsimd.affine_select(
+            out=sel[:], in_=sel[:], pattern=[[-BLOCK_PARTITIONS, 3], [0, I_PER_PASS], [-1, BLOCK_PARTITIONS]],
+            compare_op=mybir.AluOpType.is_equal, fill=0.0, base=-BLOCK_PARTITIONS, channel_multiplier=1,
+        )
+
+        def g_to_tensor(c, m):
+            quantise_g(c, m)
+            multiply(c, m)
+
+        def leave(copy, m, h):
+            r_cols = slice(h * R_HALF, (h + 1) * R_HALF)
+            copy(out=result[m][:, r_cols], in_=acc[m][:, r_cols])
+            nc.sync.dma_start(out=out[m * M_TILE : (m + 1) * M_TILE, r_cols], in_=result[m][:, r_cols])
 
         for c in range(PASSES):
             for h in range(HALVES):
-                make_p(c, h)
-            for m in range(M_TILES):
-                regroup_g(c, m)
-            for h in range(HALVES):
-                quantise_p(c, h)
-            for m in range(M_TILES):
-                quantise_g(c, m)
-                multiply(c, m)
+                double_a(on_scalar, c, h)
+        for c in range(PASSES):
+            for m in range(M_TILES - 1):
+                regroup_g(on_scalar, c, m)
 
-        for m in range(M_TILES):
-            copy = nc.scalar.copy if m % 2 == 0 else nc.vector.tensor_copy
-            for h in range(HALVES):
-                r_cols = slice(h * R_HALF, (h + 1) * R_HALF)
-                copy(out=result[m][:, r_cols], in_=acc[m][:, r_cols])
-                nc.sync.dma_start(out=out[m * M_TILE : (m + 1) * M_TILE, r_cols], in_=result[m][:, r_cols])
+        for w in range(1, 4):
+            regroup_b_on_tensor(w)
+
+        regroup(on_vector, b_first[:], b_rep[:])
+        make_p(0, 0)
+        make_p(0, 1)
+        make_p(0, 2)
+        quantise_p(0, 0)
+        make_p(0, 3)
+        make_p(1, 0)
+        quantise_p(0, 1)
+        g_to_tensor(0, 0)
+        make_p(1, 1)
+        g_to_tensor(0, 1)
+        regroup_g(on_vector, 0, 3)
+        g_to_tensor(0, 2)
+        make_p(1, 2)
+        g_to_tensor(0, 3)
+        make_p(1, 3)
+        quantise_p(1, 0)
+        quantise_p(1, 1)
+        g_to_tensor(1, 0)
+        g_to_tensor(1, 1)
+        regroup_g(on_vector, 1, 3)
+        g_to_tensor(1, 2)
+        g_to_tensor(1, 3)
+
+        leave(on_scalar, 0, 0)
+        leave(on_scalar, 0, 1)
+        leave(on_vector, 2, 0)
+        leave(on_scalar, 1, 0)
+        leave(on_vector, 3, 0)
+        leave(on_scalar, 1, 1)
+        leave(on_vector, 3, 1)
+        leave(on_scalar, 2, 1)

@@ -83,10 +83,7 @@ def tile_recon_loss_pa_s_kernel(tc, X, A, B, C, grad_out, out):
             )
 
         def regroup(copy, grouped, raw):
-            copy(
-                out=grouped.rearrange("p (n i) t -> p n t i", i=4),
-                in_=raw.rearrange("p t (n i) -> p n t i", i=4),
-            )
+            copy(out=grouped, in_=raw.rearrange("p t k -> p k t"))
 
         def regroup_g(copy, c, m):
             m_cols = slice(m * M_TILE, (m + 1) * M_TILE)

@@ -39,6 +39,7 @@ def tile_recon_loss_pa_s_kernel(tc, X, A, B, C, grad_out, out):
         a_pairs = [keep.tile([P, R, 2], BF16, name="a_pairs%d" % c) for c in range(PASSES)]
         b_rep = keep.tile([P, PACK, R_QUARTER], BF16, name="b_rep")
         b_rows = keep.tile([P, PACK, R_QUARTER], BF16, name="b_rows")
+        b_rows_grouped = keep.tile([P, R_QUARTER, PACK], BF16, name="b_rows_grouped")
         sel = keep.tile([P, 3 * P], BF16, name="sel")
         b_first = keep.tile([P, R_QUARTER, PACK], BF16, name="b_first")
         b_psum = [psum.tile([P, R_HALF, PACK], BF16, name="b_psum%d" % w) for w in range(1, 4)]
@@ -93,7 +94,7 @@ def tile_recon_loss_pa_s_kernel(tc, X, A, B, C, grad_out, out):
             nc.tensor.matmul(
                 out=b_psum[w - 1][:, 0:R_QUARTER, :],
                 lhsT=sel[:, (w - 1) * P : w * P],
-                rhs=b_rows[:].rearrange("p t r -> p r t"),
+                rhs=b_rows_grouped[:],
                 start=True,
                 stop=True,
             )
@@ -142,8 +143,8 @@ def tile_recon_loss_pa_s_kernel(tc, X, A, B, C, grad_out, out):
                 stop=(c == PASSES - 1),
             )
 
-        load_a(0)
         load_b_rows()
+        load_a(0)
         load_b_first_quarter()
         load_a(1)
         load_g(0)
@@ -175,6 +176,7 @@ def tile_recon_loss_pa_s_kernel(tc, X, A, B, C, grad_out, out):
             for m in range(M_TILES - 1):
                 regroup_g(on_scalar, c, m)
 
+        regroup(on_vector, b_rows_grouped[:], b_rows[:])
         for w in range(1, 4):
             regroup_b_on_tensor(w)
 

@@ -172,9 +172,10 @@ def tile_recon_loss_pa_s_kernel(tc, X, A, B, C, grad_out, out):
         for c in range(PASSES):
             for h in range(HALVES):
                 double_a(on_scalar, c, h)
-        for c in range(PASSES):
-            for m in range(M_TILES - 1):
-                regroup_g(on_scalar, c, m)
+        for m_pair in ((0, 1), (2,)):
+            for c in range(PASSES):
+                for m in m_pair:
+                    regroup_g(on_scalar, c, m)
 
         regroup(on_vector, b_rows_grouped[:], b_rows[:])
         for w in range(1, 4):
@@ -190,25 +191,25 @@ def tile_recon_loss_pa_s_kernel(tc, X, A, B, C, grad_out, out):
         quantise_p(0, 1)
         g_to_tensor(0, 0)
         make_p(1, 1)
-        g_to_tensor(0, 1)
-        regroup_g(on_vector, 0, 3)
-        g_to_tensor(0, 2)
         make_p(1, 2)
-        g_to_tensor(0, 3)
+        g_to_tensor(0, 1)
         make_p(1, 3)
         quantise_p(1, 0)
         quantise_p(1, 1)
         g_to_tensor(1, 0)
         g_to_tensor(1, 1)
+        regroup_g(on_vector, 0, 3)
         regroup_g(on_vector, 1, 3)
+        g_to_tensor(0, 2)
+        g_to_tensor(0, 3)
         g_to_tensor(1, 2)
         g_to_tensor(1, 3)
 
         leave(on_scalar, 0, 0)
         leave(on_scalar, 0, 1)
-        leave(on_vector, 2, 0)
         leave(on_scalar, 1, 0)
-        leave(on_vector, 3, 0)
         leave(on_scalar, 1, 1)
-        leave(on_vector, 3, 1)
+        leave(on_scalar, 2, 0)
+        leave(on_vector, 3, 0)
         leave(on_scalar, 2, 1)
+        leave(on_vector, 3, 1)

@@ -201,15 +201,15 @@ def tile_recon_loss_pa_s_kernel(tc, X, A, B, C, grad_out, out):
         regroup_g(on_vector, 0, 3)
         regroup_g(on_vector, 1, 3)
         g_to_tensor(0, 2)
-        g_to_tensor(0, 3)
         g_to_tensor(1, 2)
+        g_to_tensor(0, 3)
         g_to_tensor(1, 3)
 
         leave(on_scalar, 0, 0)
         leave(on_scalar, 0, 1)
         leave(on_scalar, 1, 0)
         leave(on_scalar, 1, 1)
-        leave(on_scalar, 2, 0)
-        leave(on_vector, 3, 0)
+        leave(on_vector, 2, 0)
         leave(on_scalar, 2, 1)
+        leave(on_vector, 3, 0)
         leave(on_vector, 3, 1)

@@ -212,4 +212,7 @@ def tile_recon_loss_pa_s_kernel(tc, X, A, B, C, grad_out, out):
         leave(on_vector, 2, 0)
         leave(on_scalar, 2, 1)
         leave(on_vector, 3, 0)
-        leave(on_vector, 3, 1)
+        for w in (2, 3):
+            r_cols = slice(w * R_QUARTER, (w + 1) * R_QUARTER)
+            nc.vector.tensor_copy(out=result[3][:, r_cols], in_=acc[3][:, r_cols])
+            nc.sync.dma_start(out=out[3 * M_TILE : 4 * M_TILE, r_cols], in_=result[3][:, r_cols])

@@ -21,6 +21,8 @@ M_TILES = N3 // M_TILE
 HALVES = 2
 R_HALF = R // HALVES
 R_QUARTER = R // 4
+PAIR = 2
+PAIRS = N2 // PAIR
 
 FLOPS = 2 * N1 * N2 * N3 * R
 BYTES = 2 * (N1 * R + N2 * R + N1 * N2 * N3) + 4 * N3 * R
@@ -38,9 +40,9 @@ def tile_recon_loss_pa_s_kernel(tc, X, A, B, C, grad_out, out):
         a_rep = [keep.tile([P, R], BF16, name="a_rep%d" % c) for c in range(PASSES)]
         a_pairs = [keep.tile([P, R, 2], BF16, name="a_pairs%d" % c) for c in range(PASSES)]
         b_rep = keep.tile([P, PACK, R_QUARTER], BF16, name="b_rep")
-        b_rows = keep.tile([P, PACK, R_QUARTER], BF16, name="b_rows")
-        b_rows_grouped = keep.tile([P, R_QUARTER, PACK], BF16, name="b_rows_grouped")
-        sel = keep.tile([P, 3 * P], BF16, name="sel")
+        b_pairs = keep.tile([P, PAIR, R], BF16, name="b_pairs")
+        b_pairs_grouped = keep.tile([P, R - R_QUARTER, PAIR], BF16, name="b_pairs_grouped")
+        sel = keep.tile([P, PACK // PAIR, P], BF16, name="sel")
         b_first = keep.tile([P, R_QUARTER, PACK], BF16, name="b_first")
         b_psum = [psum.tile([P, R_HALF, PACK], BF16, name="b_psum%d" % w) for w in range(1, 4)]
         g_raw = [keep.tile([P, PACK, N3], BF16, name="g_raw%d" % c) for c in range(PASSES)]
@@ -75,7 +77,7 @@ def tile_recon_loss_pa_s_kernel(tc, X, A, B, C, grad_out, out):
             )
 
         def load_b_rows():
-            nc.sync.dma_start(out=b_rows[0:32], in_=B.rearrange("(s t) (w r) -> w s t r", t=PACK, w=4))
+            nc.sync.dma_start(out=b_pairs[0:PAIRS], in_=B.rearrange("(q e) r -> q e r", e=PAIR))
 
         def load_g(c):
             nc.sync.dma_start(
@@ -91,13 +93,14 @@ def tile_recon_loss_pa_s_kernel(tc, X, A, B, C, grad_out, out):
             regroup(copy, g_grouped[c][:, m_cols, :], g_raw[c][:, :, m_cols])
 
         def regroup_b_on_tensor(w):
-            nc.tensor.matmul(
-                out=b_psum[w - 1][:, 0:R_QUARTER, :],
-                lhsT=sel[:, (w - 1) * P : w * P],
-                rhs=b_rows_grouped[:],
-                start=True,
-                stop=True,
-            )
+            for u in range(PACK // PAIR):
+                nc.tensor.matmul(
+                    out=b_psum[w - 1][:, 0:R_QUARTER, u * PAIR : (u + 1) * PAIR],
+                    lhsT=sel[:, u],
+                    rhs=b_pairs_grouped[:, (w - 1) * R_QUARTER : w * R_QUARTER, :],
+                    start=True,
+                    stop=True,
+                )
 
         def make_p(c, w):
             r_cols = slice(w * R_QUARTER, (w + 1) * R_QUARTER)
@@ -152,12 +155,11 @@ def tile_recon_loss_pa_s_kernel(tc, X, A, B, C, grad_out, out):
 
         on_scalar, on_vector = nc.scalar.copy, nc.vector.tensor_copy
 
-        nc.vector.memset(b_rows[32:64], 0.0)
-        nc.vector.memset(b_rows[64:128], 0.0)
+        nc.vector.memset(b_pairs_grouped[:], 0.0)
         nc.gpsimd.memset(sel[:], 1.0)
         nc.gpsimd.affine_select(
-            out=sel[:], in_=sel[:], pattern=[[-BLOCK_PARTITIONS, 3], [0, I_PER_PASS], [-1, BLOCK_PARTITIONS]],
-            compare_op=mybir.AluOpType.is_equal, fill=0.0, base=-BLOCK_PARTITIONS, channel_multiplier=1,
+            out=sel[:], in_=sel[:], pattern=[[-1, PACK // PAIR], [0, I_PER_PASS], [-PACK // PAIR, BLOCK_PARTITIONS]],
+            compare_op=mybir.AluOpType.is_equal, fill=0.0, base=0, channel_multiplier=1,
         )
 
         def g_to_tensor(c, m):
@@ -177,7 +179,13 @@ def tile_recon_loss_pa_s_kernel(tc, X, A, B, C, grad_out, out):
                 for m in m_pair:
                     regroup_g(on_scalar, c, m)
 
-        regroup(on_vector, b_rows_grouped[:], b_rows[:])
+        for w, columns in ((1, R_QUARTER), (2, 2 * R_QUARTER)):
+            r_first = w * R_QUARTER
+            regroup(
+                on_vector,
+                b_pairs_grouped[0:PAIRS, r_first - R_QUARTER : r_first - R_QUARTER + columns, :],
+                b_pairs[0:PAIRS, :, r_first : r_first + columns],
+            )
         for w in range(1, 4):
             regroup_b_on_tensor(w)
 

@@ -166,9 +166,12 @@ def tile_recon_loss_pa_s_kernel(tc, X, A, B, C, grad_out, out):
             quantise_g(c, m)
             multiply(c, m)
 
-        def leave(copy, m, h):
-            r_cols = slice(h * R_HALF, (h + 1) * R_HALF)
+        def empty(copy, m, r_first, columns):
+            r_cols = slice(r_first, r_first + columns)
             copy(out=result[m][:, r_cols], in_=acc[m][:, r_cols])
+
+        def store(m, r_first, columns):
+            r_cols = slice(r_first, r_first + columns)
             nc.sync.dma_start(out=out[m * M_TILE : (m + 1) * M_TILE, r_cols], in_=result[m][:, r_cols])
 
         for c in range(PASSES):
@@ -213,14 +216,13 @@ def tile_recon_loss_pa_s_kernel(tc, X, A, B, C, grad_out, out):
         g_to_tensor(0, 3)
         g_to_tensor(1, 3)
 
-        leave(on_scalar, 0, 0)
-        leave(on_scalar, 0, 1)
-        leave(on_scalar, 1, 0)
-        leave(on_scalar, 1, 1)
-        leave(on_vector, 2, 0)
-        leave(on_scalar, 2, 1)
-        leave(on_vector, 3, 0)
-        for w in (2, 3):
-            r_cols = slice(w * R_QUARTER, (w + 1) * R_QUARTER)
-            nc.vector.tensor_copy(out=result[3][:, r_cols], in_=acc[3][:, r_cols])
-            nc.sync.dma_start(out=out[3 * M_TILE : 4 * M_TILE, r_cols], in_=result[3][:, r_cols])
+        for r_first, columns in ((0, R_QUARTER), (R_QUARTER, R_QUARTER), (R_HALF, R_HALF)):
+            empty(on_scalar, 0, r_first, columns)
+            store(0, r_first, columns)
+        for m in (1, 2):
+            for h in range(HALVES):
+                empty(on_scalar, m, h * R_HALF, R_HALF)
+            store(m, 0, R)
+        for h in range(HALVES):
+            empty(on_vector, 3, h * R_HALF, R_HALF)
+            store(3, h * R_HALF, R_HALF)

@@ -44,7 +44,7 @@ def tile_recon_loss_pa_s_kernel(tc, X, A, B, C, grad_out, out):
         b_pairs_grouped = keep.tile([P, R - R_QUARTER, PAIR], BF16, name="b_pairs_grouped")
         sel = keep.tile([P, PACK // PAIR, P], BF16, name="sel")
         b_first = keep.tile([P, R_QUARTER, PACK], BF16, name="b_first")
-        b_psum = [psum.tile([P, R_HALF, PACK], BF16, name="b_psum%d" % w) for w in range(1, 4)]
+        b_psum = [psum.tile([P, PACK, R_QUARTER, PAIR], BF16, name="b_psum%d" % w) for w in range(1, 4)]
         g_raw = [keep.tile([P, PACK, N3], BF16, name="g_raw%d" % c) for c in range(PASSES)]
         g_grouped = [
             keep.tile([P, N3, PACK], BF16, name="g_grouped%d" % c, align_bytes=64) for c in range(PASSES)
@@ -95,7 +95,7 @@ def tile_recon_loss_pa_s_kernel(tc, X, A, B, C, grad_out, out):
         def regroup_b_on_tensor(w):
             for u in range(PACK // PAIR):
                 nc.tensor.matmul(
-                    out=b_psum[w - 1][:, 0:R_QUARTER, u * PAIR : (u + 1) * PAIR],
+                    out=b_psum[w - 1][:, u],
                     lhsT=sel[:, u],
                     rhs=b_pairs_grouped[:, (w - 1) * R_QUARTER : w * R_QUARTER, :],
                     start=True,
@@ -104,11 +104,14 @@ def tile_recon_loss_pa_s_kernel(tc, X, A, B, C, grad_out, out):
 
         def make_p(c, w):
             r_cols = slice(w * R_QUARTER, (w + 1) * R_QUARTER)
-            b_grouped = b_first[:] if w == 0 else b_psum[w - 1][:, 0:R_QUARTER, :]
+            if w == 0:
+                b_grouped = b_first[:].rearrange("p r (u e) -> p r u e", e=PAIR)
+            else:
+                b_grouped = b_psum[w - 1][:, 0 : PACK // PAIR].rearrange("p u r e -> p r u e")
             nc.vector.tensor_tensor(
                 out=p_grouped[c][:, r_cols, :].rearrange("p r (u e) -> p r u e", e=2),
                 in0=a_pairs[c][:, r_cols, :].unsqueeze(2).to_broadcast([P, R_QUARTER, PACK // 2, 2]),
-                in1=b_grouped.rearrange("p r (u e) -> p r u e", e=2),
+                in1=b_grouped,
                 op=mybir.AluOpType.mult,
             )
 

@@ -169,12 +169,9 @@ def tile_recon_loss_pa_s_kernel(tc, X, A, B, C, grad_out, out):
             quantise_g(c, m)
             multiply(c, m)
 
-        def empty(copy, m, r_first, columns):
+        def leave(copy, m, r_first, columns):
             r_cols = slice(r_first, r_first + columns)
             copy(out=result[m][:, r_cols], in_=acc[m][:, r_cols])
-
-        def store(m, r_first, columns):
-            r_cols = slice(r_first, r_first + columns)
             nc.sync.dma_start(out=out[m * M_TILE : (m + 1) * M_TILE, r_cols], in_=result[m][:, r_cols])
 
         for c in range(PASSES):
@@ -212,20 +209,16 @@ def tile_recon_loss_pa_s_kernel(tc, X, A, B, C, grad_out, out):
         quantise_p(1, 1)
         g_to_tensor(1, 0)
         g_to_tensor(1, 1)
-        regroup_g(on_vector, 0, 3)
-        regroup_g(on_vector, 1, 3)
-        g_to_tensor(0, 2)
-        g_to_tensor(1, 2)
-        g_to_tensor(0, 3)
-        g_to_tensor(1, 3)
+        for c in range(PASSES):
+            g_to_tensor(c, 2)
+            regroup_g(on_vector, c, 3)
+        for c in range(PASSES):
+            g_to_tensor(c, 3)
 
         for r_first, columns in ((0, R_QUARTER), (R_QUARTER, R_QUARTER), (R_HALF, R_HALF)):
-            empty(on_scalar, 0, r_first, columns)
-            store(0, r_first, columns)
-        for m in (1, 2):
-            for h in range(HALVES):
-                empty(on_scalar, m, h * R_HALF, R_HALF)
-            store(m, 0, R)
+            leave(on_scalar, 0, r_first, columns)
         for h in range(HALVES):
-            empty(on_vector, 3, h * R_HALF, R_HALF)
-            store(3, h * R_HALF, R_HALF)
+            leave(on_scalar, 1, h * R_HALF, R_HALF)
+            leave(on_vector, 2, h * R_HALF, R_HALF)
+        for h in range(HALVES):
+            leave(on_vector, 3, h * R_HALF, R_HALF)

@@ -193,8 +193,8 @@ def tile_recon_loss_pa_s_kernel(tc, X, A, B, C, grad_out, out):
             regroup_b_on_tensor(w)
 
         regroup(on_vector, b_first[:], b_rep[:])
-        make_p(0, 0)
         make_p(0, 1)
+        make_p(0, 0)
         make_p(0, 2)
         quantise_p(0, 0)
         make_p(0, 3)

from contextlib import ExitStack

import concourse.mybir as mybir

BF16 = mybir.dt.bfloat16
F32 = mybir.dt.float32
U32 = mybir.dt.uint32
U8 = mybir.dt.uint8
E4M3_X4 = mybir.dt.float8_e4m3fn_x4
E5M2_X4 = mybir.dt.float8_e5m2_x4

N1, N2, N3, R = 32, 32, 512, 512
P = 128
PACK = 4
K_PASS = P * PACK
PASSES = N1 * N2 // K_PASS
BLOCK_PARTITIONS = 8
I_PER_PASS = P // BLOCK_PARTITIONS
M_TILE = 128
M_TILES = N3 // M_TILE
HALVES = 2
R_HALF = R // HALVES
R_QUARTER = R // 4
PAIR = 2
PAIRS = N2 // PAIR

FLOPS = 2 * N1 * N2 * N3 * R
BYTES = 2 * (N1 * R + N2 * R + N1 * N2 * N3) + 4 * N3 * R


def tile_recon_loss_pa_s_kernel(tc, X, A, B, C, grad_out, out):
    nc = tc.nc
    g_rows = grad_out.rearrange("i j k -> (i j) k")

    with ExitStack() as ctx:
        keep = ctx.enter_context(tc.tile_pool(name="keep", bufs=1))
        psum = ctx.enter_context(tc.psum_pool(name="psum", bufs=1))
        ctx.enter_context(tc.manual_schedule())

        a_rep = [keep.tile([P, R], BF16, name="a_rep%d" % c) for c in range(PASSES)]
        a_pairs = [keep.tile([P, R, 2], BF16, name="a_pairs%d" % c) for c in range(PASSES)]
        b_rep = keep.tile([P, PACK, R_QUARTER], BF16, name="b_rep")
        b_pairs = keep.tile([P, PAIR, R], BF16, name="b_pairs")
        b_pairs_grouped = keep.tile([P, R - R_QUARTER, PAIR], BF16, name="b_pairs_grouped")
        sel = keep.tile([P, PACK // PAIR, P], BF16, name="sel")
        b_first = keep.tile([P, R_QUARTER, PACK], BF16, name="b_first")
        b_psum = [psum.tile([P, PACK, R_QUARTER, PAIR], BF16, name="b_psum%d" % w) for w in range(1, 4)]
        g_raw = [keep.tile([P, PACK, N3], BF16, name="g_raw%d" % c) for c in range(PASSES)]
        g_grouped = [
            keep.tile([P, N3, PACK], BF16, name="g_grouped%d" % c, align_bytes=64) for c in range(PASSES)
        ]
        p_grouped = [
            keep.tile([P, R, PACK], BF16, name="p_grouped%d" % c, align_bytes=64) for c in range(PASSES)
        ]
        p_codes = [keep.tile([P, R], U32, name="p_codes%d" % c, align_bytes=64) for c in range(PASSES)]
        p_scales = [keep.tile([P, R], U8, name="p_scales%d" % c, align_bytes=64) for c in range(PASSES)]
        g_codes = [keep.tile([P, N3], U32, name="g_codes%d" % c, align_bytes=64) for c in range(PASSES)]
        g_scales = [keep.tile([P, N3], U8, name="g_scales%d" % c, align_bytes=64) for c in range(PASSES)]
        acc = [psum.tile([M_TILE, R], F32, name="acc%d" % m) for m in range(M_TILES)]
        result = [keep.tile([M_TILE, R], F32, name="result%d" % m) for m in range(M_TILES)]

        def load_a(c):
            nc.sync.dma_start(
                out=a_rep[c][:],
                in_=A[c * I_PER_PASS : (c + 1) * I_PER_PASS, :]
                .unsqueeze(1)
                .to_broadcast([I_PER_PASS, BLOCK_PARTITIONS, R]),
            )

        def load_b_first_quarter():
            nc.sync.dma_start(
                out=b_rep[:],
                in_=B[:, 0:R_QUARTER]
                .rearrange("(s t) r -> s t r", t=PACK)
                .unsqueeze(0)
                .to_broadcast([I_PER_PASS, BLOCK_PARTITIONS, PACK, R_QUARTER]),
            )

        def load_b_rows():
            nc.sync.dma_start(out=b_pairs[0:PAIRS], in_=B.rearrange("(q e) r -> q e r", e=PAIR))

        def load_g(c):
            nc.sync.dma_start(
                out=g_raw[c][:],
                in_=g_rows[c * K_PASS : (c + 1) * K_PASS, :].rearrange("(p t) k -> p t k", t=PACK),
            )

        def regroup(copy, grouped, raw):
            copy(out=grouped, in_=raw.rearrange("p t k -> p k t"))

        def regroup_g(copy, c, m):
            m_cols = slice(m * M_TILE, (m + 1) * M_TILE)
            regroup(copy, g_grouped[c][:, m_cols, :], g_raw[c][:, :, m_cols])

        def regroup_b_on_tensor(w):
            for u in range(PACK // PAIR):
                nc.tensor.matmul(
                    out=b_psum[w - 1][:, u],
                    lhsT=sel[:, u],
                    rhs=b_pairs_grouped[:, (w - 1) * R_QUARTER : w * R_QUARTER, :],
                    start=True,
                    stop=True,
                )

        def make_p(c, w):
            r_cols = slice(w * R_QUARTER, (w + 1) * R_QUARTER)
            if w == 0:
                b_grouped = b_first[:].rearrange("p r (u e) -> p r u e", e=PAIR)
            else:
                b_grouped = b_psum[w - 1][:, 0 : PACK // PAIR].rearrange("p u r e -> p r u e")
            nc.vector.tensor_tensor(
                out=p_grouped[c][:, r_cols, :].rearrange("p r (u e) -> p r u e", e=2),
                in0=a_pairs[c][:, r_cols, :].unsqueeze(2).to_broadcast([P, R_QUARTER, PACK // 2, 2]),
                in1=b_grouped,
                op=mybir.AluOpType.mult,
            )

        def double_a(copy, c, h):
            r_cols = slice(h * R_HALF, (h + 1) * R_HALF)
            copy(
                out=a_pairs[c][:, r_cols, :], in_=a_rep[c][:, r_cols].unsqueeze(2).to_broadcast([P, R_HALF, 2])
            )

        def quantise_p(c, h):
            r_cols = slice(h * R_HALF, (h + 1) * R_HALF)
            nc.vector.quantize_mx(
                out=p_codes[c][:, r_cols].bitcast(E4M3_X4),
                scales=p_scales[c][:, r_cols],
                in_=p_grouped[c][:, r_cols, :].rearrange("p r t -> p (r t)"),
            )

        def quantise_g(c, m):
            m_cols = slice(m * M_TILE, (m + 1) * M_TILE)
            nc.vector.quantize_mx(
                out=g_codes[c][:, m_cols].bitcast(E5M2_X4),
                scales=g_scales[c][:, m_cols],
                in_=g_grouped[c][:, m_cols, :].rearrange("p k t -> p (k t)"),
            )

        def multiply(c, m):
            m_cols = slice(m * M_TILE, (m + 1) * M_TILE)
            nc.tensor.matmul_mx(
                out=acc[m][:],
                lhsT=g_codes[c][:, m_cols].bitcast(E5M2_X4),
                lhsT_scale=g_scales[c][:, m_cols],
                rhs=p_codes[c][:].bitcast(E4M3_X4),
                rhs_scale=p_scales[c][:],
                start=(c == 0),
                stop=(c == PASSES - 1),
            )

        load_b_rows()
        load_a(0)
        load_b_first_quarter()
        load_a(1)
        load_g(0)
        load_g(1)

        on_scalar, on_vector = nc.scalar.copy, nc.vector.tensor_copy

        nc.vector.memset(b_pairs_grouped[:], 0.0)
        nc.gpsimd.memset(sel[:], 1.0)
        nc.gpsimd.affine_select(
            out=sel[:], in_=sel[:], pattern=[[-1, PACK // PAIR], [0, I_PER_PASS], [-PACK // PAIR, BLOCK_PARTITIONS]],
            compare_op=mybir.AluOpType.is_equal, fill=0.0, base=0, channel_multiplier=1,
        )

        def g_to_tensor(c, m):
            quantise_g(c, m)
            multiply(c, m)

        def leave(copy, m, r_first, columns):
            r_cols = slice(r_first, r_first + columns)
            copy(out=result[m][:, r_cols], in_=acc[m][:, r_cols])
            nc.sync.dma_start(out=out[m * M_TILE : (m + 1) * M_TILE, r_cols], in_=result[m][:, r_cols])

        for c in range(PASSES):
            for h in range(HALVES):
                double_a(on_scalar, c, h)
        for m_pair in ((0, 1), (2,)):
            for c in range(PASSES):
                for m in m_pair:
                    regroup_g(on_scalar, c, m)

        for w, columns in ((1, R_QUARTER), (2, 2 * R_QUARTER)):
            r_first = w * R_QUARTER
            regroup(
                on_vector,
                b_pairs_grouped[0:PAIRS, r_first - R_QUARTER : r_first - R_QUARTER + columns, :],
                b_pairs[0:PAIRS, :, r_first : r_first + columns],
            )
        for w in range(1, 4):
            regroup_b_on_tensor(w)

        regroup(on_vector, b_first[:], b_rep[:])
        make_p(0, 1)
        make_p(0, 0)
        make_p(0, 2)
        quantise_p(0, 0)
        make_p(0, 3)
        make_p(1, 0)
        quantise_p(0, 1)
        g_to_tensor(0, 0)
        make_p(1, 1)
        make_p(1, 2)
        g_to_tensor(0, 1)
        make_p(1, 3)
        quantise_p(1, 0)
        quantise_p(1, 1)
        g_to_tensor(1, 0)
        g_to_tensor(1, 1)
        for c in range(PASSES):
            g_to_tensor(c, 2)
            regroup_g(on_vector, c, 3)
        for c in range(PASSES):
            g_to_tensor(c, 3)

        for r_first, columns in ((0, R_QUARTER), (R_QUARTER, R_QUARTER), (R_HALF, R_HALF)):
            leave(on_scalar, 0, r_first, columns)
        for h in range(HALVES):
            leave(on_scalar, 1, h * R_HALF, R_HALF)
            leave(on_vector, 2, h * R_HALF, R_HALF)
        for h in range(HALVES):
            leave(on_vector, 3, h * R_HALF, R_HALF)
